import numpy as np
import ml_dtypes


def mxq(x, axis, fmt="e4m3"):
    dtype, down = {"e4m3": (ml_dtypes.float8_e4m3fn, 7), "e5m2": (ml_dtypes.float8_e5m2, 14)}[fmt]
    v = np.moveaxis(np.asarray(x, np.float32).astype(ml_dtypes.bfloat16).astype(np.float64), axis, -1)
    blocks = v.reshape(v.shape[:-1] + (-1, 32))
    amax = np.abs(blocks).max(-1, keepdims=True)
    byte = np.maximum(np.where(amax > 0, np.frexp(amax)[1] - 1 + 127, 0) - down, 1)
    scale = np.exp2(byte - 127.0)
    codes = (blocks / scale).astype(np.float32).astype(dtype).astype(np.float64)
    return np.moveaxis((codes * scale).reshape(v.shape), -1, axis)


WIDE = False


def mx_kscale(k):
    if not WIDE:
        return np.ones(k)
    levels = np.array([10, -10, 5, -5, 0])
    a = np.random.permutation(np.resize(levels, k // 512 * 4)).reshape(k // 512, 4)
    idx = np.arange(k)
    return np.exp2(a[idx // 512, idx % 128 // 32])


BF16 = ml_dtypes.bfloat16


def bf(x):
    return np.asarray(x, np.float32).astype(BF16)


def f64(x):
    return np.asarray(x).astype(np.float64)


B, HD, F = 256, 2048, 4096
STEP = 0.1


def setup_inputs():
    s = mx_kscale(HD)
    return {"u_old": bf(np.random.standard_normal((B, HD)) * s),
            "v_old": bf(np.random.standard_normal((B, HD)) / s),
            "W1": bf(np.random.standard_normal((F, HD)) * np.sqrt(6.0 / (HD + F)) / s),
            "b1": bf(np.random.standard_normal(F) * 0.5)}


def reference(u_old, v_old, W1, b1):
    w = f64(W1)
    v_mid = np.tanh((mxq(f64(u_old), 1, "e4m3") @ mxq(w, 1, "e4m3").T) + f64(b1))
    v_sig = mxq(v_mid, 1, "e4m3") @ mxq(w, 0, "e4m3")
    return f64(v_old) + STEP * v_sig

@@ -1,0 +1,210 @@
+from contextlib import ExitStack
+
+import concourse.mybir as mybir
+from concourse.masks import make_identity
+
+F32 = mybir.dt.float32
+BF16 = mybir.dt.bfloat16
+U32 = mybir.dt.uint32
+U8 = mybir.dt.uint8
+FP8X4 = mybir.dt.float8_e4m3fn_x4
+TANH = mybir.ActivationFunctionType.Tanh
+MULT = mybir.AluOpType.mult
+ADD = mybir.AluOpType.add
+
+B, HD, F = 256, 2048, 4096
+STEP = 0.1
+FLOPS = 2 * 2 * B * HD * F
+
+P = 128
+PACK = 4
+K_PASS = P * PACK
+B_TILES = B // P
+H_PASSES = HD // K_PASS
+CHUNKS = F // K_PASS
+F_TILES = CHUNKS * PACK
+PAIRS = F_TILES // 2
+N_TILE = 512
+H_BLOCKS = HD // N_TILE
+STEPS = CHUNKS * H_BLOCKS
+ROW_WORDS = HD // 2
+
+
+def tile_invblock_pa_kernel(tc, u_old, v_old, W1, b1, out):
+    nc = tc.nc
+    with ExitStack() as ctx:
+        ctx.enter_context(tc.manual_schedule())
+        weights = ctx.enter_context(tc.tile_pool(name="weights", bufs=1))
+        keep = ctx.enter_context(tc.tile_pool(name="keep", bufs=1))
+        stage2 = ctx.enter_context(tc.tile_pool(name="stage2", bufs=4))
+
+        ident = keep.tile([P, P], F32)
+        make_identity(nc, ident[:])
+        u_sb = keep.tile([P, B_TILES, HD], BF16)
+        nc.sync.dma_start(out=u_sb[:], in_=u_old.rearrange("(t p) h -> p t h", p=P))
+        bias_bf = keep.tile([P, CHUNKS, PACK], BF16)
+        nc.scalar.dma_start(out=bias_bf[:], in_=b1.rearrange("(g p j) -> p g j", p=P, j=PACK))
+        w_sb = []
+        for g in range(CHUNKS):
+            w = weights.tile([P, PACK, HD], BF16, name="w%d" % g)
+            rows = W1[g * K_PASS : (g + 1) * K_PASS, :].rearrange("(p j) h -> p j h", j=PACK)
+            for first in range(0, PACK, 2):
+                nc.sync.dma_start(out=w[:, first : first + 2, :], in_=rows[:, first : first + 2, :])
+            w_sb.append(w)
+        v_sb = keep.tile([P, B_TILES, HD], BF16)
+        nc.sync.dma_start(out=v_sb[:], in_=v_old.rearrange("(t p) h -> p t h", p=P))
+
+        u_codes = keep.tile([P, H_PASSES * B], U32, align_bytes=64)
+        u_scales = keep.tile([P, H_PASSES * B], U8, align_bytes=64)
+        v_codes = keep.tile([P, CHUNKS, B], U32, align_bytes=64)
+        v_scales = keep.tile([P, CHUNKS, B], U8, align_bytes=64)
+        bias = keep.tile([P, F_TILES], F32)
+
+        with ExitStack() as phase1:
+            stage1 = phase1.enter_context(tc.tile_pool(name="stage1", bufs=4))
+            hidden_sb = phase1.enter_context(tc.tile_pool(name="hidden_sb", bufs=2))
+            psum_t = phase1.enter_context(tc.psum_pool(name="psum_t", bufs=6))
+            psum_h = phase1.enter_context(tc.psum_pool(name="psum_h", bufs=2))
+
+            def transpose_rows(rows):
+                words = rows.bitcast(F32)
+                banks = []
+                for half in range(2):
+                    bank = psum_t.tile([P, 2, 2, P], F32)
+                    for c2 in range(2):
+                        for u in range(2):
+                            first = ((2 * half + c2) * 2 + u) * P
+                            nc.tensor.transpose(bank[:, c2, u, :], words[:, first : first + P], ident[:])
+                    banks.append(bank)
+                return banks
+
+            def empty_banks(banks, dests):
+                for k in range(4):
+                    copy = nc.vector.tensor_copy if k == 3 else nc.scalar.copy
+                    copy(out=dests[k], in_=banks[k][:].rearrange("q c u r -> q c r u"))
+
+            u_banks = transpose_rows(u_sb[:, 0, :]) + transpose_rows(u_sb[:, 1, :])
+            u_pieces = []
+            for half in range(2):
+                grouped = stage1.tile([P, PACK * N_TILE], BF16, align_bytes=64)
+                u_pieces.append(grouped)
+            u_views = [
+                piece[:].bitcast(F32).rearrange("q (c t r u) -> q c t r u", c=2, t=B_TILES, u=2)
+                for piece in u_pieces
+            ]
+            empty_banks(u_banks, [u_views[half][:, :, t, :, :] for t in range(B_TILES) for half in range(2)])
+            for half in range(2):
+                cols = slice(half * N_TILE, (half + 1) * N_TILE)
+                nc.vector.quantize_mx(
+                    out=u_codes[:, cols].bitcast(FP8X4), scales=u_scales[:, cols], in_=u_pieces[half][:]
+                )
+            nc.vector.tensor_copy(out=bias[:], in_=bias_bf[:].rearrange("p g j -> p (g j)"))
+
+            def prepare_pair(r):
+                banks, dests, pieces = [], [], []
+                for i in (2 * r, 2 * r + 1):
+                    g, j = divmod(i, PACK)
+                    banks.extend(transpose_rows(w_sb[g][:, j, :]))
+                for i in range(2):
+                    grouped = stage1.tile([P, PACK * N_TILE], BF16, align_bytes=64)
+                    view = grouped[:].bitcast(F32).rearrange("q (c r u) -> q c r u", c=H_PASSES, u=2)
+                    dests.extend([view[:, 0:2, :, :], view[:, 2:4, :, :]])
+                    pieces.append(grouped)
+                empty_banks(banks, dests)
+                operands = []
+                for grouped in pieces:
+                    w_codes = stage1.tile([P, H_PASSES * P], U32, align_bytes=64)
+                    w_scales = stage1.tile([P, H_PASSES * P], U8, align_bytes=64)
+                    nc.vector.quantize_mx(out=w_codes[:].bitcast(FP8X4), scales=w_scales[:], in_=grouped[:])
+                    operands.append((w_codes, w_scales))
+                return operands
+
+            def hidden_tile(i, operand, act):
+                w_codes, w_scales = operand
+                hid = psum_h.tile([P, B], F32)
+                for c in range(H_PASSES):
+                    f_cols = slice(c * P, (c + 1) * P)
+                    b_cols = slice(c * B, (c + 1) * B)
+                    nc.tensor.matmul_mx(
+                        out=hid[:],
+                        lhsT=w_codes[:, f_cols].bitcast(FP8X4),
+                        lhsT_scale=w_scales[:, f_cols],
+                        rhs=u_codes[:, b_cols].bitcast(FP8X4),
+                        rhs_scale=u_scales[:, b_cols],
+                        start=(c == 0),
+                        stop=(c == H_PASSES - 1),
+                    )
+                nc.scalar.activation(out=act[:, i % PACK, :], in_=hid[:], func=TANH, bias=bias[:, i : i + 1], scale=1.0)
+
+            ready = prepare_pair(0)
+            for r in range(PAIRS):
+                coming = prepare_pair(r + 1) if r + 1 < PAIRS else None
+                g = r // 2
+                if r % 2 == 0:
+                    act = hidden_sb.tile([P, PACK, B], BF16)
+                hidden_tile(2 * r, ready[0], act)
+                hidden_tile(2 * r + 1, ready[1], act)
+                ready = coming
+                if r % 2 == 1:
+                    v_grouped = hidden_sb.tile([P, B, PACK], BF16, align_bytes=64)
+                    nc.vector.tensor_copy(
+                        out=v_grouped[:].rearrange("p (c i) t -> p c t i", i=4),
+                        in_=act[:].rearrange("p t (c i) -> p c t i", i=4),
+                    )
+                    nc.vector.quantize_mx(
+                        out=v_codes[:, g, :].bitcast(FP8X4),
+                        scales=v_scales[:, g, :],
+                        in_=v_grouped[:].rearrange("p b t -> p (b t)"),
+                    )
+
+        results = ctx.enter_context(tc.tile_pool(name="results", bufs=B_TILES * H_BLOCKS))
+        psum_acc = ctx.enter_context(tc.psum_pool(name="psum_acc", bufs=1))
+        acc = [
+            [psum_acc.tile([P, N_TILE], F32, name="acc%d%d" % (t, n)) for n in range(H_BLOCKS)]
+            for t in range(B_TILES)
+        ]
+
+        def regroup(s):
+            g, n = divmod(s, H_BLOCKS)
+            grouped = stage2.tile([P, N_TILE, PACK], BF16, align_bytes=64)
+            copy = nc.vector.tensor_copy if n % 2 == 0 else nc.scalar.copy
+            copy(
+                out=grouped[:].rearrange("p (c i) t -> p c t i", i=4),
+                in_=w_sb[g][:, :, n * N_TILE : (n + 1) * N_TILE].rearrange("p t (c i) -> p c t i", i=4),
+            )
+            return grouped
+
+        def finish(n):
+            h_cols = slice(n * N_TILE, (n + 1) * N_TILE)
+            for t in range(B_TILES):
+                res = results.tile([P, N_TILE], F32)
+                nc.vector.scalar_tensor_tensor(
+                    out=res[:], in0=acc[t][n][:], scalar=STEP, in1=v_sb[:, t, h_cols], op0=MULT, op1=ADD
+                )
+                nc.sync.dma_start(out=out[t * P : (t + 1) * P, h_cols], in_=res[:])
+
+        grouped_of = {0: regroup(0), 1: regroup(1)}
+        for s in range(STEPS):
+            g, n = divmod(s, H_BLOCKS)
+            if s + 2 < STEPS:
+                grouped_of[s + 2] = regroup(s + 2)
+            w_codes = stage2.tile([P, N_TILE], U32, align_bytes=64)
+            w_scales = stage2.tile([P, N_TILE], U8, align_bytes=64)
+            nc.vector.quantize_mx(
+                out=w_codes[:].bitcast(FP8X4),
+                scales=w_scales[:],
+                in_=grouped_of[s][:].rearrange("p h t -> p (h t)"),
+            )
+            for t in range(B_TILES):
+                nc.tensor.matmul_mx(
+                    out=acc[t][n][:],
+                    lhsT=v_codes[:, g, t * P : (t + 1) * P].bitcast(FP8X4),
+                    lhsT_scale=v_scales[:, g, t * P : (t + 1) * P],
+                    rhs=w_codes[:].bitcast(FP8X4),
+                    rhs_scale=w_scales[:],
+                    start=(g == 0),
+                    stop=(g == CHUNKS - 1),
+                )
+            if g == CHUNKS - 1 and n > 0:
+                finish(n - 1)
+        finish(H_BLOCKS - 1)

@@ -27,38 +27,81 @@ PAIRS = F_TILES // 2
 N_TILE = 512
 H_BLOCKS = HD // N_TILE
 STEPS = CHUNKS * H_BLOCKS
-ROW_WORDS = HD // 2
+EARLY_STEPS = STEPS // 2
+HALF_TILE = N_TILE // 2
+CHUNKS_AHEAD = 4
+
+
+def step_place(k):
+    place, n = divmod(k, H_BLOCKS)
+    g = 2 * place if k < EARLY_STEPS else 2 * (place - CHUNKS // 2) + 1
+    return g, n
 
 
 def tile_invblock_pa_kernel(tc, u_old, v_old, W1, b1, out):
     nc = tc.nc
     with ExitStack() as ctx:
         ctx.enter_context(tc.manual_schedule())
-        weights = ctx.enter_context(tc.tile_pool(name="weights", bufs=1))
+        passing = ctx.enter_context(tc.tile_pool(name="passing", bufs=2))
+        staying = ctx.enter_context(tc.tile_pool(name="staying", bufs=CHUNKS // 2))
         keep = ctx.enter_context(tc.tile_pool(name="keep", bufs=1))
         stage2 = ctx.enter_context(tc.tile_pool(name="stage2", bufs=4))
 
         ident = keep.tile([P, P], F32)
         make_identity(nc, ident[:])
         u_sb = keep.tile([P, B_TILES, HD], BF16)
-        nc.sync.dma_start(out=u_sb[:], in_=u_old.rearrange("(t p) h -> p t h", p=P))
+        for t in range(B_TILES):
+            nc.sync.dma_start(out=u_sb[:, t, :], in_=u_old[t * P : (t + 1) * P, :])
         bias_bf = keep.tile([P, CHUNKS, PACK], BF16)
         nc.scalar.dma_start(out=bias_bf[:], in_=b1.rearrange("(g p j) -> p g j", p=P, j=PACK))
-        w_sb = []
-        for g in range(CHUNKS):
-            w = weights.tile([P, PACK, HD], BF16, name="w%d" % g)
+        warm = keep.tile([P, 1], F32)
+        nc.scalar.activation(out=warm[:], in_=ident[:, 0:1], func=TANH)
+        w_sb = {}
+
+        def load_chunk(g):
+            pool = passing if g % 2 == 0 else staying
+            w = pool.tile([P, PACK, HD], BF16)
             rows = W1[g * K_PASS : (g + 1) * K_PASS, :].rearrange("(p j) h -> p j h", j=PACK)
             for first in range(0, PACK, 2):
                 nc.sync.dma_start(out=w[:, first : first + 2, :], in_=rows[:, first : first + 2, :])
-            w_sb.append(w)
-        v_sb = keep.tile([P, B_TILES, HD], BF16)
-        nc.sync.dma_start(out=v_sb[:], in_=v_old.rearrange("(t p) h -> p t h", p=P))
+            w_sb[g] = w
+
+        for g in range(CHUNKS_AHEAD):
+            load_chunk(g)
 
         u_codes = keep.tile([P, H_PASSES * B], U32, align_bytes=64)
         u_scales = keep.tile([P, H_PASSES * B], U8, align_bytes=64)
         v_codes = keep.tile([P, CHUNKS, B], U32, align_bytes=64)
         v_scales = keep.tile([P, CHUNKS, B], U8, align_bytes=64)
         bias = keep.tile([P, F_TILES], F32)
+        early_codes = keep.tile([P, EARLY_STEPS, N_TILE], U32, align_bytes=64)
+        early_scales = keep.tile([P, EARLY_STEPS, N_TILE], U8, align_bytes=64)
+
+        grouped_of = {}
+        operand_of = {}
+
+        def regroup(k):
+            g, n = step_place(k)
+            rows = w_sb[g][:, :, n * N_TILE : (n + 1) * N_TILE]
+            grouped = stage2.tile([P, N_TILE, PACK], BF16, align_bytes=64)
+            for copy, cols in ((nc.vector.tensor_copy, slice(0, HALF_TILE)), (nc.scalar.copy, slice(HALF_TILE, N_TILE))):
+                copy(
+                    out=grouped[:, cols, :].rearrange("p (c i) t -> p c t i", i=4),
+                    in_=rows[:, :, cols].rearrange("p t (c i) -> p c t i", i=4),
+                )
+            grouped_of[k] = grouped
+
+        def quantise_step(k):
+            if k < EARLY_STEPS:
+                codes, scales = early_codes[:, k, :], early_scales[:, k, :]
+            else:
+                late_codes = stage2.tile([P, N_TILE], U32, align_bytes=64)
+                late_scales = stage2.tile([P, N_TILE], U8, align_bytes=64)
+                codes, scales = late_codes[:], late_scales[:]
+            nc.vector.quantize_mx(
+                out=codes.bitcast(FP8X4), scales=scales, in_=grouped_of[k][:].rearrange("p h t -> p (h t)")
+            )
+            operand_of[k] = (codes, scales)
 
         with ExitStack() as phase1:
             stage1 = phase1.enter_context(tc.tile_pool(name="stage1", bufs=4))
@@ -100,7 +143,7 @@ def tile_invblock_pa_kernel(tc, u_old, v_old, W1, b1, out):
                 )
             nc.vector.tensor_copy(out=bias[:], in_=bias_bf[:].rearrange("p g j -> p (g j)"))
 
-            def prepare_pair(r):
+            def transpose_pair(r):
                 banks, dests, pieces = [], [], []
                 for i in (2 * r, 2 * r + 1):
                     g, j = divmod(i, PACK)
@@ -111,6 +154,9 @@ def tile_invblock_pa_kernel(tc, u_old, v_old, W1, b1, out):
                     dests.extend([view[:, 0:2, :, :], view[:, 2:4, :, :]])
                     pieces.append(grouped)
                 empty_banks(banks, dests)
+                return pieces
+
+            def quantise_pair(pieces):
                 operands = []
                 for grouped in pieces:
                     w_codes = stage1.tile([P, H_PASSES * P], U32, align_bytes=64)
@@ -136,26 +182,38 @@ def tile_invblock_pa_kernel(tc, u_old, v_old, W1, b1, out):
                     )
                 nc.scalar.activation(out=act[:, i % PACK, :], in_=hid[:], func=TANH, bias=bias[:, i : i + 1], scale=1.0)
 
-            ready = prepare_pair(0)
+            ready = quantise_pair(transpose_pair(0))
             for r in range(PAIRS):
-                coming = prepare_pair(r + 1) if r + 1 < PAIRS else None
-                g = r // 2
-                if r % 2 == 0:
+                g, second_pair = divmod(r, 2)
+                if r + 1 < PAIRS:
+                    pieces = transpose_pair(r + 1)
+                if r > 0:
+                    quantise_step(r - 1)
+                if r + 1 < PAIRS:
+                    coming = quantise_pair(pieces)
+                if not second_pair:
                     act = hidden_sb.tile([P, PACK, B], BF16)
                 hidden_tile(2 * r, ready[0], act)
                 hidden_tile(2 * r + 1, ready[1], act)
                 ready = coming
-                if r % 2 == 1:
+                if second_pair:
                     v_grouped = hidden_sb.tile([P, B, PACK], BF16, align_bytes=64)
                     nc.vector.tensor_copy(
                         out=v_grouped[:].rearrange("p (c i) t -> p c t i", i=4),
                         in_=act[:].rearrange("p t (c i) -> p c t i", i=4),
                     )
+                regroup(r)
+                if second_pair:
                     nc.vector.quantize_mx(
                         out=v_codes[:, g, :].bitcast(FP8X4),
                         scales=v_scales[:, g, :],
                         in_=v_grouped[:].rearrange("p b t -> p (b t)"),
                     )
+                if r % H_BLOCKS == H_BLOCKS - 1:
+                    for later in range(g + CHUNKS_AHEAD - 1, min(g + CHUNKS_AHEAD + 1, CHUNKS)):
+                        load_chunk(later)
+            v_sb = keep.tile([P, B_TILES, HD], BF16)
+            nc.sync.dma_start(out=v_sb[:], in_=v_old.rearrange("(t p) h -> p t h", p=P))
 
         results = ctx.enter_context(tc.tile_pool(name="results", bufs=B_TILES * H_BLOCKS))
         psum_acc = ctx.enter_context(tc.psum_pool(name="psum_acc", bufs=1))
@@ -163,16 +221,6 @@ def tile_invblock_pa_kernel(tc, u_old, v_old, W1, b1, out):
             [psum_acc.tile([P, N_TILE], F32, name="acc%d%d" % (t, n)) for n in range(H_BLOCKS)]
             for t in range(B_TILES)
         ]
-
-        def regroup(s):
-            g, n = divmod(s, H_BLOCKS)
-            grouped = stage2.tile([P, N_TILE, PACK], BF16, align_bytes=64)
-            copy = nc.vector.tensor_copy if n % 2 == 0 else nc.scalar.copy
-            copy(
-                out=grouped[:].rearrange("p (c i) t -> p c t i", i=4),
-                in_=w_sb[g][:, :, n * N_TILE : (n + 1) * N_TILE].rearrange("p t (c i) -> p c t i", i=4),
-            )
-            return grouped
 
         def finish(n):
             h_cols = slice(n * N_TILE, (n + 1) * N_TILE)
@@ -183,28 +231,30 @@ def tile_invblock_pa_kernel(tc, u_old, v_old, W1, b1, out):
                 )
                 nc.sync.dma_start(out=out[t * P : (t + 1) * P, h_cols], in_=res[:])
 
-        grouped_of = {0: regroup(0), 1: regroup(1)}
-        for s in range(STEPS):
-            g, n = divmod(s, H_BLOCKS)
-            if s + 2 < STEPS:
-                grouped_of[s + 2] = regroup(s + 2)
-            w_codes = stage2.tile([P, N_TILE], U32, align_bytes=64)
-            w_scales = stage2.tile([P, N_TILE], U8, align_bytes=64)
-            nc.vector.quantize_mx(
-                out=w_codes[:].bitcast(FP8X4),
-                scales=w_scales[:],
-                in_=grouped_of[s][:].rearrange("p h t -> p (h t)"),
-            )
+        def second_matmul(k):
+            g, n = step_place(k)
+            codes, scales = operand_of[k]
             for t in range(B_TILES):
                 nc.tensor.matmul_mx(
                     out=acc[t][n][:],
                     lhsT=v_codes[:, g, t * P : (t + 1) * P].bitcast(FP8X4),
                     lhsT_scale=v_scales[:, g, t * P : (t + 1) * P],
-                    rhs=w_codes[:].bitcast(FP8X4),
-                    rhs_scale=w_scales[:],
+                    rhs=codes.bitcast(FP8X4),
+                    rhs_scale=scales,
                     start=(g == 0),
                     stop=(g == CHUNKS - 1),
                 )
+
+        quantise_step(EARLY_STEPS - 1)
+        regroup(EARLY_STEPS)
+        for k in range(EARLY_STEPS):
+            second_matmul(k)
+        for k in range(EARLY_STEPS, STEPS):
+            if k + 1 < STEPS:
+                regroup(k + 1)
+            quantise_step(k)
+            second_matmul(k)
+            g, n = step_place(k)
             if g == CHUNKS - 1 and n > 0:
                 finish(n - 1)
         finish(H_BLOCKS - 1)

@@ -28,14 +28,17 @@ N_TILE = 512
 H_BLOCKS = HD // N_TILE
 STEPS = CHUNKS * H_BLOCKS
 EARLY_STEPS = STEPS // 2
-HALF_TILE = N_TILE // 2
+VECTOR_COLS_PHASE1 = 448
+VECTOR_COLS_PHASE2 = 192
 CHUNKS_AHEAD = 4
 
 
 def step_place(k):
-    place, n = divmod(k, H_BLOCKS)
-    g = 2 * place if k < EARLY_STEPS else 2 * (place - CHUNKS // 2) + 1
-    return g, n
+    if k < EARLY_STEPS:
+        place, n = divmod(k, H_BLOCKS)
+        return 2 * place, n
+    n, place = divmod(k - EARLY_STEPS, CHUNKS // 2)
+    return 2 * place + 1, n
 
 
 def tile_invblock_pa_kernel(tc, u_old, v_old, W1, b1, out):
@@ -84,7 +87,8 @@ def tile_invblock_pa_kernel(tc, u_old, v_old, W1, b1, out):
             g, n = step_place(k)
             rows = w_sb[g][:, :, n * N_TILE : (n + 1) * N_TILE]
             grouped = stage2.tile([P, N_TILE, PACK], BF16, align_bytes=64)
-            for copy, cols in ((nc.vector.tensor_copy, slice(0, HALF_TILE)), (nc.scalar.copy, slice(HALF_TILE, N_TILE))):
+            split = VECTOR_COLS_PHASE1 if k < EARLY_STEPS else VECTOR_COLS_PHASE2
+            for copy, cols in ((nc.vector.tensor_copy, slice(0, split)), (nc.scalar.copy, slice(split, N_TILE))):
                 copy(
                     out=grouped[:, cols, :].rearrange("p (c i) t -> p c t i", i=4),
                     in_=rows[:, :, cols].rearrange("p t (c i) -> p c t i", i=4),
@@ -122,9 +126,8 @@ def tile_invblock_pa_kernel(tc, u_old, v_old, W1, b1, out):
                 return banks
 
             def empty_banks(banks, dests):
-                for k in range(4):
-                    copy = nc.vector.tensor_copy if k == 3 else nc.scalar.copy
-                    copy(out=dests[k], in_=banks[k][:].rearrange("q c u r -> q c r u"))
+                for bank, dest in zip(banks, dests):
+                    nc.scalar.copy(out=dest, in_=bank[:].rearrange("q c u r -> q c r u"))
 
             u_banks = transpose_rows(u_sb[:, 0, :]) + transpose_rows(u_sb[:, 1, :])
             u_pieces = []
@@ -156,14 +159,11 @@ def tile_invblock_pa_kernel(tc, u_old, v_old, W1, b1, out):
                 empty_banks(banks, dests)
                 return pieces
 
-            def quantise_pair(pieces):
-                operands = []
-                for grouped in pieces:
-                    w_codes = stage1.tile([P, H_PASSES * P], U32, align_bytes=64)
-                    w_scales = stage1.tile([P, H_PASSES * P], U8, align_bytes=64)
-                    nc.vector.quantize_mx(out=w_codes[:].bitcast(FP8X4), scales=w_scales[:], in_=grouped[:])
-                    operands.append((w_codes, w_scales))
-                return operands
+            def quantise_tile(grouped):
+                w_codes = stage1.tile([P, H_PASSES * P], U32, align_bytes=64)
+                w_scales = stage1.tile([P, H_PASSES * P], U8, align_bytes=64)
+                nc.vector.quantize_mx(out=w_codes[:].bitcast(FP8X4), scales=w_scales[:], in_=grouped[:])
+                return w_codes, w_scales
 
             def hidden_tile(i, operand, act):
                 w_codes, w_scales = operand
@@ -182,36 +182,51 @@ def tile_invblock_pa_kernel(tc, u_old, v_old, W1, b1, out):
                     )
                 nc.scalar.activation(out=act[:, i % PACK, :], in_=hid[:], func=TANH, bias=bias[:, i : i + 1], scale=1.0)
 
-            ready = quantise_pair(transpose_pair(0))
+            v_grouped_of = {}
+
+            def regroup_hidden(g, act):
+                v_grouped = hidden_sb.tile([P, B, PACK], BF16, align_bytes=64)
+                nc.vector.tensor_copy(
+                    out=v_grouped[:].rearrange("p (c i) t -> p c t i", i=4),
+                    in_=act[:].rearrange("p t (c i) -> p c t i", i=4),
+                )
+                v_grouped_of[g] = v_grouped
+
+            def quantise_hidden(g):
+                nc.vector.quantize_mx(
+                    out=v_codes[:, g, :].bitcast(FP8X4),
+                    scales=v_scales[:, g, :],
+                    in_=v_grouped_of[g][:].rearrange("p b t -> p (b t)"),
+                )
+
+            pieces = transpose_pair(0)
+            ready = [quantise_tile(pieces[0]), quantise_tile(pieces[1])]
             for r in range(PAIRS):
                 g, second_pair = divmod(r, 2)
                 if r + 1 < PAIRS:
                     pieces = transpose_pair(r + 1)
+                if g > 0 and not second_pair:
+                    quantise_hidden(g - 1)
                 if r > 0:
                     quantise_step(r - 1)
+                coming = []
                 if r + 1 < PAIRS:
-                    coming = quantise_pair(pieces)
+                    coming.append(quantise_tile(pieces[0]))
+                regroup(r)
+                if r + 1 < PAIRS:
+                    coming.append(quantise_tile(pieces[1]))
                 if not second_pair:
                     act = hidden_sb.tile([P, PACK, B], BF16)
                 hidden_tile(2 * r, ready[0], act)
                 hidden_tile(2 * r + 1, ready[1], act)
                 ready = coming
                 if second_pair:
-                    v_grouped = hidden_sb.tile([P, B, PACK], BF16, align_bytes=64)
-                    nc.vector.tensor_copy(
-                        out=v_grouped[:].rearrange("p (c i) t -> p c t i", i=4),
-                        in_=act[:].rearrange("p t (c i) -> p c t i", i=4),
-                    )
-                regroup(r)
-                if second_pair:
-                    nc.vector.quantize_mx(
-                        out=v_codes[:, g, :].bitcast(FP8X4),
-                        scales=v_scales[:, g, :],
-                        in_=v_grouped[:].rearrange("p b t -> p (b t)"),
-                    )
+                    regroup_hidden(g, act)
                 if r % H_BLOCKS == H_BLOCKS - 1:
                     for later in range(g + CHUNKS_AHEAD - 1, min(g + CHUNKS_AHEAD + 1, CHUNKS)):
                         load_chunk(later)
+            quantise_step(EARLY_STEPS - 1)
+            quantise_hidden(CHUNKS - 1)
             v_sb = keep.tile([P, B_TILES, HD], BF16)
             nc.sync.dma_start(out=v_sb[:], in_=v_old.rearrange("(t p) h -> p t h", p=P))
 
@@ -245,16 +260,16 @@ def tile_invblock_pa_kernel(tc, u_old, v_old, W1, b1, out):
                     stop=(g == CHUNKS - 1),
                 )
 
-        quantise_step(EARLY_STEPS - 1)
         regroup(EARLY_STEPS)
-        for k in range(EARLY_STEPS):
-            second_matmul(k)
         for k in range(EARLY_STEPS, STEPS):
+            g, n = step_place(k)
+            if g == 1:
+                for early in range(n, EARLY_STEPS, H_BLOCKS):
+                    second_matmul(early)
             if k + 1 < STEPS:
                 regroup(k + 1)
             quantise_step(k)
             second_matmul(k)
-            g, n = step_place(k)
-            if g == CHUNKS - 1 and n > 0:
+            if g == 1 and n > 0:
                 finish(n - 1)
         finish(H_BLOCKS - 1)

@@ -28,8 +28,7 @@ N_TILE = 512
 H_BLOCKS = HD // N_TILE
 STEPS = CHUNKS * H_BLOCKS
 EARLY_STEPS = STEPS // 2
-VECTOR_COLS_PHASE1 = 448
-VECTOR_COLS_PHASE2 = 192
+VECTOR_COLS_LATE = 192
 CHUNKS_AHEAD = 4
 
 
@@ -87,8 +86,11 @@ def tile_invblock_pa_kernel(tc, u_old, v_old, W1, b1, out):
             g, n = step_place(k)
             rows = w_sb[g][:, :, n * N_TILE : (n + 1) * N_TILE]
             grouped = stage2.tile([P, N_TILE, PACK], BF16, align_bytes=64)
-            split = VECTOR_COLS_PHASE1 if k < EARLY_STEPS else VECTOR_COLS_PHASE2
-            for copy, cols in ((nc.vector.tensor_copy, slice(0, split)), (nc.scalar.copy, slice(split, N_TILE))):
+            vector_cols = N_TILE if k < EARLY_STEPS else VECTOR_COLS_LATE
+            shares = [(nc.vector.tensor_copy, slice(0, vector_cols))]
+            if vector_cols < N_TILE:
+                shares.append((nc.scalar.copy, slice(vector_cols, N_TILE)))
+            for copy, cols in shares:
                 copy(
                     out=grouped[:, cols, :].rearrange("p (c i) t -> p c t i", i=4),
                     in_=rows[:, :, cols].rearrange("p t (c i) -> p c t i", i=4),
@@ -108,7 +110,7 @@ def tile_invblock_pa_kernel(tc, u_old, v_old, W1, b1, out):
             operand_of[k] = (codes, scales)
 
         with ExitStack() as phase1:
-            stage1 = phase1.enter_context(tc.tile_pool(name="stage1", bufs=4))
+            stage1 = phase1.enter_context(tc.tile_pool(name="stage1", bufs=2))
             hidden_sb = phase1.enter_context(tc.tile_pool(name="hidden_sb", bufs=2))
             psum_t = phase1.enter_context(tc.psum_pool(name="psum_t", bufs=6))
             psum_h = phase1.enter_context(tc.psum_pool(name="psum_h", bufs=2))
@@ -130,38 +132,25 @@ def tile_invblock_pa_kernel(tc, u_old, v_old, W1, b1, out):
                     nc.scalar.copy(out=dest, in_=bank[:].rearrange("q c u r -> q c r u"))
 
             u_banks = transpose_rows(u_sb[:, 0, :]) + transpose_rows(u_sb[:, 1, :])
-            u_pieces = []
-            for half in range(2):
-                grouped = stage1.tile([P, PACK * N_TILE], BF16, align_bytes=64)
-                u_pieces.append(grouped)
-            u_views = [
-                piece[:].bitcast(F32).rearrange("q (c t r u) -> q c t r u", c=2, t=B_TILES, u=2)
-                for piece in u_pieces
-            ]
-            empty_banks(u_banks, [u_views[half][:, :, t, :, :] for t in range(B_TILES) for half in range(2)])
-            for half in range(2):
-                cols = slice(half * N_TILE, (half + 1) * N_TILE)
-                nc.vector.quantize_mx(
-                    out=u_codes[:, cols].bitcast(FP8X4), scales=u_scales[:, cols], in_=u_pieces[half][:]
-                )
+            grouped = stage1.tile([P, 2 * PACK * N_TILE], BF16, align_bytes=64)
+            u_view = grouped[:].bitcast(F32).rearrange("q (c t r u) -> q c t r u", c=H_PASSES, t=B_TILES, u=2)
+            empty_banks(u_banks, [u_view[:, first : first + 2, t, :, :] for t in range(B_TILES) for first in (0, 2)])
+            nc.vector.quantize_mx(out=u_codes[:].bitcast(FP8X4), scales=u_scales[:], in_=grouped[:])
             nc.vector.tensor_copy(out=bias[:], in_=bias_bf[:].rearrange("p g j -> p (g j)"))
 
             def transpose_pair(r):
-                banks, dests, pieces = [], [], []
+                banks = []
                 for i in (2 * r, 2 * r + 1):
                     g, j = divmod(i, PACK)
                     banks.extend(transpose_rows(w_sb[g][:, j, :]))
-                for i in range(2):
-                    grouped = stage1.tile([P, PACK * N_TILE], BF16, align_bytes=64)
-                    view = grouped[:].bitcast(F32).rearrange("q (c r u) -> q c r u", c=H_PASSES, u=2)
-                    dests.extend([view[:, 0:2, :, :], view[:, 2:4, :, :]])
-                    pieces.append(grouped)
-                empty_banks(banks, dests)
-                return pieces
+                grouped = stage1.tile([P, 2 * PACK * N_TILE], BF16, align_bytes=64)
+                view = grouped[:].bitcast(F32).rearrange("q (i c r u) -> q i c r u", i=2, c=H_PASSES, u=2)
+                empty_banks(banks, [view[:, i, first : first + 2, :, :] for i in range(2) for first in (0, 2)])
+                return grouped
 
-            def quantise_tile(grouped):
-                w_codes = stage1.tile([P, H_PASSES * P], U32, align_bytes=64)
-                w_scales = stage1.tile([P, H_PASSES * P], U8, align_bytes=64)
+            def quantise_pair(grouped):
+                w_codes = stage1.tile([P, 2 * H_PASSES * P], U32, align_bytes=64)
+                w_scales = stage1.tile([P, 2 * H_PASSES * P], U8, align_bytes=64)
                 nc.vector.quantize_mx(out=w_codes[:].bitcast(FP8X4), scales=w_scales[:], in_=grouped[:])
                 return w_codes, w_scales
 
@@ -169,7 +158,8 @@ def tile_invblock_pa_kernel(tc, u_old, v_old, W1, b1, out):
                 w_codes, w_scales = operand
                 hid = psum_h.tile([P, B], F32)
                 for c in range(H_PASSES):
-                    f_cols = slice(c * P, (c + 1) * P)
+                    first = ((i % 2) * H_PASSES + c) * P
+                    f_cols = slice(first, first + P)
                     b_cols = slice(c * B, (c + 1) * B)
                     nc.tensor.matmul_mx(
                         out=hid[:],
@@ -199,26 +189,22 @@ def tile_invblock_pa_kernel(tc, u_old, v_old, W1, b1, out):
                     in_=v_grouped_of[g][:].rearrange("p b t -> p (b t)"),
                 )
 
-            pieces = transpose_pair(0)
-            ready = [quantise_tile(pieces[0]), quantise_tile(pieces[1])]
+            ready = quantise_pair(transpose_pair(0))
             for r in range(PAIRS):
                 g, second_pair = divmod(r, 2)
                 if r + 1 < PAIRS:
-                    pieces = transpose_pair(r + 1)
+                    grouped = transpose_pair(r + 1)
                 if g > 0 and not second_pair:
                     quantise_hidden(g - 1)
                 if r > 0:
                     quantise_step(r - 1)
-                coming = []
-                if r + 1 < PAIRS:
-                    coming.append(quantise_tile(pieces[0]))
                 regroup(r)
                 if r + 1 < PAIRS:
-                    coming.append(quantise_tile(pieces[1]))
+                    coming = quantise_pair(grouped)
                 if not second_pair:
                     act = hidden_sb.tile([P, PACK, B], BF16)
-                hidden_tile(2 * r, ready[0], act)
-                hidden_tile(2 * r + 1, ready[1], act)
+                hidden_tile(2 * r, ready, act)
+                hidden_tile(2 * r + 1, ready, act)
                 ready = coming
                 if second_pair:
                     regroup_hidden(g, act)

@@ -24,17 +24,18 @@ H_PASSES = HD // K_PASS
 CHUNKS = F // K_PASS
 F_TILES = CHUNKS * PACK
 PAIRS = F_TILES // 2
-N_TILE = 512
-H_BLOCKS = HD // N_TILE
-STEPS = CHUNKS * H_BLOCKS
+PANEL = 512
+PANELS = HD // PANEL
+STEPS = CHUNKS * PANELS
 EARLY_STEPS = STEPS // 2
-VECTOR_COLS_LATE = 192
 CHUNKS_AHEAD = 4
+VECTOR_COLS_PHASE1 = 448
+VECTOR_COLS_PHASE2 = 192
 
 
 def step_place(k):
     if k < EARLY_STEPS:
-        place, n = divmod(k, H_BLOCKS)
+        place, n = divmod(k, PANELS)
         return 2 * place, n
     n, place = divmod(k - EARLY_STEPS, CHUNKS // 2)
     return 2 * place + 1, n
@@ -76,21 +77,18 @@ def tile_invblock_pa_kernel(tc, u_old, v_old, W1, b1, out):
         v_codes = keep.tile([P, CHUNKS, B], U32, align_bytes=64)
         v_scales = keep.tile([P, CHUNKS, B], U8, align_bytes=64)
         bias = keep.tile([P, F_TILES], F32)
-        early_codes = keep.tile([P, EARLY_STEPS, N_TILE], U32, align_bytes=64)
-        early_scales = keep.tile([P, EARLY_STEPS, N_TILE], U8, align_bytes=64)
+        early_codes = keep.tile([P, EARLY_STEPS, PANEL], U32, align_bytes=64)
+        early_scales = keep.tile([P, EARLY_STEPS, PANEL], U8, align_bytes=64)
 
         grouped_of = {}
         operand_of = {}
 
         def regroup(k):
             g, n = step_place(k)
-            rows = w_sb[g][:, :, n * N_TILE : (n + 1) * N_TILE]
-            grouped = stage2.tile([P, N_TILE, PACK], BF16, align_bytes=64)
-            vector_cols = N_TILE if k < EARLY_STEPS else VECTOR_COLS_LATE
-            shares = [(nc.vector.tensor_copy, slice(0, vector_cols))]
-            if vector_cols < N_TILE:
-                shares.append((nc.scalar.copy, slice(vector_cols, N_TILE)))
-            for copy, cols in shares:
+            rows = w_sb[g][:, :, n * PANEL : (n + 1) * PANEL]
+            grouped = stage2.tile([P, PANEL, PACK], BF16, align_bytes=64)
+            split = VECTOR_COLS_PHASE1 if k < EARLY_STEPS else VECTOR_COLS_PHASE2
+            for copy, cols in ((nc.vector.tensor_copy, slice(0, split)), (nc.scalar.copy, slice(split, PANEL))):
                 copy(
                     out=grouped[:, cols, :].rearrange("p (c i) t -> p c t i", i=4),
                     in_=rows[:, :, cols].rearrange("p t (c i) -> p c t i", i=4),
@@ -101,8 +99,8 @@ def tile_invblock_pa_kernel(tc, u_old, v_old, W1, b1, out):
             if k < EARLY_STEPS:
                 codes, scales = early_codes[:, k, :], early_scales[:, k, :]
             else:
-                late_codes = stage2.tile([P, N_TILE], U32, align_bytes=64)
-                late_scales = stage2.tile([P, N_TILE], U8, align_bytes=64)
+                late_codes = stage2.tile([P, PANEL], U32, align_bytes=64)
+                late_scales = stage2.tile([P, PANEL], U8, align_bytes=64)
                 codes, scales = late_codes[:], late_scales[:]
             nc.vector.quantize_mx(
                 out=codes.bitcast(FP8X4), scales=scales, in_=grouped_of[k][:].rearrange("p h t -> p (h t)")
@@ -110,7 +108,7 @@ def tile_invblock_pa_kernel(tc, u_old, v_old, W1, b1, out):
             operand_of[k] = (codes, scales)
 
         with ExitStack() as phase1:
-            stage1 = phase1.enter_context(tc.tile_pool(name="stage1", bufs=2))
+            stage1 = phase1.enter_context(tc.tile_pool(name="stage1", bufs=4))
             hidden_sb = phase1.enter_context(tc.tile_pool(name="hidden_sb", bufs=2))
             psum_t = phase1.enter_context(tc.psum_pool(name="psum_t", bufs=6))
             psum_h = phase1.enter_context(tc.psum_pool(name="psum_h", bufs=2))
@@ -132,25 +130,38 @@ def tile_invblock_pa_kernel(tc, u_old, v_old, W1, b1, out):
                     nc.scalar.copy(out=dest, in_=bank[:].rearrange("q c u r -> q c r u"))
 
             u_banks = transpose_rows(u_sb[:, 0, :]) + transpose_rows(u_sb[:, 1, :])
-            grouped = stage1.tile([P, 2 * PACK * N_TILE], BF16, align_bytes=64)
-            u_view = grouped[:].bitcast(F32).rearrange("q (c t r u) -> q c t r u", c=H_PASSES, t=B_TILES, u=2)
-            empty_banks(u_banks, [u_view[:, first : first + 2, t, :, :] for t in range(B_TILES) for first in (0, 2)])
-            nc.vector.quantize_mx(out=u_codes[:].bitcast(FP8X4), scales=u_scales[:], in_=grouped[:])
+            u_pieces = []
+            for half in range(2):
+                grouped = stage1.tile([P, PACK * PANEL], BF16, align_bytes=64)
+                u_pieces.append(grouped)
+            u_views = [
+                piece[:].bitcast(F32).rearrange("q (c t r u) -> q c t r u", c=2, t=B_TILES, u=2)
+                for piece in u_pieces
+            ]
+            empty_banks(u_banks, [u_views[half][:, :, t, :, :] for t in range(B_TILES) for half in range(2)])
+            for half in range(2):
+                cols = slice(half * PANEL, (half + 1) * PANEL)
+                nc.vector.quantize_mx(
+                    out=u_codes[:, cols].bitcast(FP8X4), scales=u_scales[:, cols], in_=u_pieces[half][:]
+                )
             nc.vector.tensor_copy(out=bias[:], in_=bias_bf[:].rearrange("p g j -> p (g j)"))
 
             def transpose_pair(r):
-                banks = []
+                banks, dests, pieces = [], [], []
                 for i in (2 * r, 2 * r + 1):
                     g, j = divmod(i, PACK)
                     banks.extend(transpose_rows(w_sb[g][:, j, :]))
-                grouped = stage1.tile([P, 2 * PACK * N_TILE], BF16, align_bytes=64)
-                view = grouped[:].bitcast(F32).rearrange("q (i c r u) -> q i c r u", i=2, c=H_PASSES, u=2)
-                empty_banks(banks, [view[:, i, first : first + 2, :, :] for i in range(2) for first in (0, 2)])
-                return grouped
+                for i in range(2):
+                    grouped = stage1.tile([P, PACK * PANEL], BF16, align_bytes=64)
+                    view = grouped[:].bitcast(F32).rearrange("q (c r u) -> q c r u", c=H_PASSES, u=2)
+                    dests.extend([view[:, 0:2, :, :], view[:, 2:4, :, :]])
+                    pieces.append(grouped)
+                empty_banks(banks, dests)
+                return pieces
 
-            def quantise_pair(grouped):
-                w_codes = stage1.tile([P, 2 * H_PASSES * P], U32, align_bytes=64)
-                w_scales = stage1.tile([P, 2 * H_PASSES * P], U8, align_bytes=64)
+            def quantise_tile(grouped):
+                w_codes = stage1.tile([P, H_PASSES * P], U32, align_bytes=64)
+                w_scales = stage1.tile([P, H_PASSES * P], U8, align_bytes=64)
                 nc.vector.quantize_mx(out=w_codes[:].bitcast(FP8X4), scales=w_scales[:], in_=grouped[:])
                 return w_codes, w_scales
 
@@ -158,8 +169,7 @@ def tile_invblock_pa_kernel(tc, u_old, v_old, W1, b1, out):
                 w_codes, w_scales = operand
                 hid = psum_h.tile([P, B], F32)
                 for c in range(H_PASSES):
-                    first = ((i % 2) * H_PASSES + c) * P
-                    f_cols = slice(first, first + P)
+                    f_cols = slice(c * P, (c + 1) * P)
                     b_cols = slice(c * B, (c + 1) * B)
                     nc.tensor.matmul_mx(
                         out=hid[:],
@@ -189,26 +199,30 @@ def tile_invblock_pa_kernel(tc, u_old, v_old, W1, b1, out):
                     in_=v_grouped_of[g][:].rearrange("p b t -> p (b t)"),
                 )
 
-            ready = quantise_pair(transpose_pair(0))
+            pieces = transpose_pair(0)
+            ready = [quantise_tile(pieces[0]), quantise_tile(pieces[1])]
             for r in range(PAIRS):
                 g, second_pair = divmod(r, 2)
                 if r + 1 < PAIRS:
-                    grouped = transpose_pair(r + 1)
-                if g > 0 and not second_pair:
-                    quantise_hidden(g - 1)
+                    pieces = transpose_pair(r + 1)
                 if r > 0:
                     quantise_step(r - 1)
+                if g > 0 and not second_pair:
+                    quantise_hidden(g - 1)
+                coming = []
+                if r + 1 < PAIRS:
+                    coming.append(quantise_tile(pieces[0]))
                 regroup(r)
                 if r + 1 < PAIRS:
-                    coming = quantise_pair(grouped)
+                    coming.append(quantise_tile(pieces[1]))
                 if not second_pair:
                     act = hidden_sb.tile([P, PACK, B], BF16)
-                hidden_tile(2 * r, ready, act)
-                hidden_tile(2 * r + 1, ready, act)
+                hidden_tile(2 * r, ready[0], act)
+                hidden_tile(2 * r + 1, ready[1], act)
                 ready = coming
                 if second_pair:
                     regroup_hidden(g, act)
-                if r % H_BLOCKS == H_BLOCKS - 1:
+                if r % PANELS == PANELS - 1:
                     for later in range(g + CHUNKS_AHEAD - 1, min(g + CHUNKS_AHEAD + 1, CHUNKS)):
                         load_chunk(later)
             quantise_step(EARLY_STEPS - 1)
@@ -216,17 +230,17 @@ def tile_invblock_pa_kernel(tc, u_old, v_old, W1, b1, out):
             v_sb = keep.tile([P, B_TILES, HD], BF16)
             nc.sync.dma_start(out=v_sb[:], in_=v_old.rearrange("(t p) h -> p t h", p=P))
 
-        results = ctx.enter_context(tc.tile_pool(name="results", bufs=B_TILES * H_BLOCKS))
+        results = ctx.enter_context(tc.tile_pool(name="results", bufs=B_TILES * PANELS))
         psum_acc = ctx.enter_context(tc.psum_pool(name="psum_acc", bufs=1))
         acc = [
-            [psum_acc.tile([P, N_TILE], F32, name="acc%d%d" % (t, n)) for n in range(H_BLOCKS)]
+            [psum_acc.tile([P, PANEL], F32, name="acc%d%d" % (t, n)) for n in range(PANELS)]
             for t in range(B_TILES)
         ]
 
         def finish(n):
-            h_cols = slice(n * N_TILE, (n + 1) * N_TILE)
+            h_cols = slice(n * PANEL, (n + 1) * PANEL)
             for t in range(B_TILES):
-                res = results.tile([P, N_TILE], F32)
+                res = results.tile([P, PANEL], F32)
                 nc.vector.scalar_tensor_tensor(
                     out=res[:], in0=acc[t][n][:], scalar=STEP, in1=v_sb[:, t, h_cols], op0=MULT, op1=ADD
                 )
@@ -250,7 +264,7 @@ def tile_invblock_pa_kernel(tc, u_old, v_old, W1, b1, out):
         for k in range(EARLY_STEPS, STEPS):
             g, n = step_place(k)
             if g == 1:
-                for early in range(n, EARLY_STEPS, H_BLOCKS):
+                for early in range(n, EARLY_STEPS, PANELS):
                     second_matmul(early)
             if k + 1 < STEPS:
                 regroup(k + 1)
@@ -258,4 +272,4 @@ def tile_invblock_pa_kernel(tc, u_old, v_old, W1, b1, out):
             second_matmul(k)
             if g == 1 and n > 0:
                 finish(n - 1)
-        finish(H_BLOCKS - 1)
+        finish(PANELS - 1)

@@ -27,18 +27,22 @@ PAIRS = F_TILES // 2
 PANEL = 512
 PANELS = HD // PANEL
 STEPS = CHUNKS * PANELS
-EARLY_STEPS = STEPS // 2
-CHUNKS_AHEAD = 4
-VECTOR_COLS_PHASE1 = 448
+PASSING = (0, 1, 3, 5)
+STAYING = (2, 4, 6, 7)
+LEAD = 3
+EARLY_STEPS = PAIRS + LEAD
+VECTOR_COLS_PHASE1 = 416
+VECTOR_COLS_FIRST = 320
 VECTOR_COLS_PHASE2 = 192
 
 
 def step_place(k):
-    if k < EARLY_STEPS:
+    passing_steps = len(PASSING) * PANELS
+    if k < passing_steps:
         place, n = divmod(k, PANELS)
-        return 2 * place, n
-    n, place = divmod(k - EARLY_STEPS, CHUNKS // 2)
-    return 2 * place + 1, n
+        return PASSING[place], n
+    n, place = divmod(k - passing_steps, len(STAYING))
+    return STAYING[place], n
 
 
 def tile_invblock_pa_kernel(tc, u_old, v_old, W1, b1, out):
@@ -46,15 +50,12 @@ def tile_invblock_pa_kernel(tc, u_old, v_old, W1, b1, out):
     with ExitStack() as ctx:
         ctx.enter_context(tc.manual_schedule())
         passing = ctx.enter_context(tc.tile_pool(name="passing", bufs=2))
-        staying = ctx.enter_context(tc.tile_pool(name="staying", bufs=CHUNKS // 2))
+        staying = ctx.enter_context(tc.tile_pool(name="staying", bufs=len(STAYING)))
         keep = ctx.enter_context(tc.tile_pool(name="keep", bufs=1))
         stage2 = ctx.enter_context(tc.tile_pool(name="stage2", bufs=4))
 
         ident = keep.tile([P, P], F32)
         make_identity(nc, ident[:])
-        u_sb = keep.tile([P, B_TILES, HD], BF16)
-        for t in range(B_TILES):
-            nc.sync.dma_start(out=u_sb[:, t, :], in_=u_old[t * P : (t + 1) * P, :])
         bias_bf = keep.tile([P, CHUNKS, PACK], BF16)
         nc.scalar.dma_start(out=bias_bf[:], in_=b1.rearrange("(g p j) -> p g j", p=P, j=PACK))
         warm = keep.tile([P, 1], F32)
@@ -62,15 +63,29 @@ def tile_invblock_pa_kernel(tc, u_old, v_old, W1, b1, out):
         w_sb = {}
 
         def load_chunk(g):
-            pool = passing if g % 2 == 0 else staying
-            w = pool.tile([P, PACK, HD], BF16)
+            pool = passing if g in PASSING else staying
             rows = W1[g * K_PASS : (g + 1) * K_PASS, :].rearrange("(p j) h -> p j h", j=PACK)
-            for first in range(0, PACK, 2):
-                nc.sync.dma_start(out=w[:, first : first + 2, :], in_=rows[:, first : first + 2, :])
+            if g == 0:
+                w = pool.tile([P, PANELS, PACK, PANEL], BF16)
+                for n in range(PANELS):
+                    nc.sync.dma_start(out=w[:, n, :, :], in_=rows[:, :, n * PANEL : (n + 1) * PANEL])
+            else:
+                w = pool.tile([P, PACK, HD], BF16)
+                for first in range(0, PACK, 2):
+                    nc.sync.dma_start(out=w[:, first : first + 2, :], in_=rows[:, first : first + 2, :])
             w_sb[g] = w
 
-        for g in range(CHUNKS_AHEAD):
-            load_chunk(g)
+        def panel_of_chunk(g, n):
+            if g == 0:
+                return w_sb[g][:, n, :, :]
+            return w_sb[g][:, :, n * PANEL : (n + 1) * PANEL]
+
+        load_chunk(0)
+        u_sb = keep.tile([P, B_TILES, HD], BF16)
+        for t in range(B_TILES):
+            nc.sync.dma_start(out=u_sb[:, t, :], in_=u_old[t * P : (t + 1) * P, :])
+        load_chunk(1)
+        load_chunk(2)
 
         u_codes = keep.tile([P, H_PASSES * B], U32, align_bytes=64)
         u_scales = keep.tile([P, H_PASSES * B], U8, align_bytes=64)
@@ -85,9 +100,9 @@ def tile_invblock_pa_kernel(tc, u_old, v_old, W1, b1, out):
 
         def regroup(k):
             g, n = step_place(k)
-            rows = w_sb[g][:, :, n * PANEL : (n + 1) * PANEL]
+            rows = panel_of_chunk(g, n)
             grouped = stage2.tile([P, PANEL, PACK], BF16, align_bytes=64)
-            split = VECTOR_COLS_PHASE1 if k < EARLY_STEPS else VECTOR_COLS_PHASE2
+            split = VECTOR_COLS_FIRST if k == 0 else VECTOR_COLS_PHASE1 if k < EARLY_STEPS else VECTOR_COLS_PHASE2
             for copy, cols in ((nc.vector.tensor_copy, slice(0, split)), (nc.scalar.copy, slice(split, PANEL))):
                 copy(
                     out=grouped[:, cols, :].rearrange("p (c i) t -> p c t i", i=4),
@@ -113,50 +128,32 @@ def tile_invblock_pa_kernel(tc, u_old, v_old, W1, b1, out):
             psum_t = phase1.enter_context(tc.psum_pool(name="psum_t", bufs=6))
             psum_h = phase1.enter_context(tc.psum_pool(name="psum_h", bufs=2))
 
-            def transpose_rows(rows):
-                words = rows.bitcast(F32)
-                banks = []
-                for half in range(2):
-                    bank = psum_t.tile([P, 2, 2, P], F32)
-                    for c2 in range(2):
-                        for u in range(2):
-                            first = ((2 * half + c2) * 2 + u) * P
-                            nc.tensor.transpose(bank[:, c2, u, :], words[:, first : first + P], ident[:])
-                    banks.append(bank)
-                return banks
+            def transpose_half(rows_of, half):
+                bank = psum_t.tile([P, 2, 2, P], F32)
+                for c2 in range(2):
+                    words = rows_of(2 * half + c2).bitcast(F32)
+                    for u in range(2):
+                        nc.tensor.transpose(bank[:, c2, u, :], words[:, u * P : (u + 1) * P], ident[:])
+                return bank
 
-            def empty_banks(banks, dests):
-                for bank, dest in zip(banks, dests):
-                    nc.scalar.copy(out=dest, in_=bank[:].rearrange("q c u r -> q c r u"))
+            def empty_bank(copy, bank, dest):
+                copy(out=dest, in_=bank[:].rearrange("q c u r -> q c r u"))
 
-            u_banks = transpose_rows(u_sb[:, 0, :]) + transpose_rows(u_sb[:, 1, :])
-            u_pieces = []
-            for half in range(2):
-                grouped = stage1.tile([P, PACK * PANEL], BF16, align_bytes=64)
-                u_pieces.append(grouped)
-            u_views = [
-                piece[:].bitcast(F32).rearrange("q (c t r u) -> q c t r u", c=2, t=B_TILES, u=2)
-                for piece in u_pieces
-            ]
-            empty_banks(u_banks, [u_views[half][:, :, t, :, :] for t in range(B_TILES) for half in range(2)])
-            for half in range(2):
-                cols = slice(half * PANEL, (half + 1) * PANEL)
-                nc.vector.quantize_mx(
-                    out=u_codes[:, cols].bitcast(FP8X4), scales=u_scales[:, cols], in_=u_pieces[half][:]
-                )
-            nc.vector.tensor_copy(out=bias[:], in_=bias_bf[:].rearrange("p g j -> p (g j)"))
-
-            def transpose_pair(r):
-                banks, dests, pieces = [], [], []
-                for i in (2 * r, 2 * r + 1):
-                    g, j = divmod(i, PACK)
-                    banks.extend(transpose_rows(w_sb[g][:, j, :]))
+            def transpose_pair(r, by_half):
+                pieces, views = [], []
                 for i in range(2):
                     grouped = stage1.tile([P, PACK * PANEL], BF16, align_bytes=64)
-                    view = grouped[:].bitcast(F32).rearrange("q (c r u) -> q c r u", c=H_PASSES, u=2)
-                    dests.extend([view[:, 0:2, :, :], view[:, 2:4, :, :]])
+                    views.append(grouped[:].bitcast(F32).rearrange("q (c r u) -> q c r u", c=H_PASSES, u=2))
                     pieces.append(grouped)
-                empty_banks(banks, dests)
+                order = [(i, half) for i in range(2) for half in range(2)]
+                if by_half:
+                    order = [(i, half) for half in range(2) for i in range(2)]
+                banks = []
+                for i, half in order:
+                    g, j = divmod(2 * r + i, PACK)
+                    banks.append(transpose_half(lambda n: panel_of_chunk(g, n)[:, j, :], half))
+                for (i, half), bank in zip(order, banks):
+                    empty_bank(nc.scalar.copy, bank, views[i][:, 2 * half : 2 * half + 2, :, :])
                 return pieces
 
             def quantise_tile(grouped):
@@ -199,20 +196,44 @@ def tile_invblock_pa_kernel(tc, u_old, v_old, W1, b1, out):
                     in_=v_grouped_of[g][:].rearrange("p b t -> p (b t)"),
                 )
 
-            pieces = transpose_pair(0)
+            regroup(0)
+            pieces = transpose_pair(0, True)
+            regroup(1)
+            quantise_step(0)
+            regroup(2)
+            quantise_step(1)
             ready = [quantise_tile(pieces[0]), quantise_tile(pieces[1])]
+
+            u_banks = []
+            for t in range(B_TILES):
+                for half in range(2):
+                    u_banks.append(transpose_half(lambda n: u_sb[:, t, n * PANEL : (n + 1) * PANEL], half))
+            u_pieces = []
+            for half in range(2):
+                grouped = stage1.tile([P, PACK * PANEL], BF16, align_bytes=64)
+                u_pieces.append(grouped)
+            for t in range(B_TILES):
+                for half, copy in enumerate((nc.scalar.copy, nc.vector.tensor_copy)):
+                    view = u_pieces[half][:].bitcast(F32).rearrange("q (c t r u) -> q c t r u", c=2, t=B_TILES, u=2)
+                    empty_bank(copy, u_banks[2 * t + half], view[:, :, t, :, :])
+            nc.vector.tensor_copy(out=bias[:], in_=bias_bf[:].rearrange("p g j -> p (g j)"))
+            for half in range(2):
+                cols = slice(half * PANEL, (half + 1) * PANEL)
+                nc.vector.quantize_mx(
+                    out=u_codes[:, cols].bitcast(FP8X4), scales=u_scales[:, cols], in_=u_pieces[half][:]
+                )
+
             for r in range(PAIRS):
                 g, second_pair = divmod(r, 2)
                 if r + 1 < PAIRS:
-                    pieces = transpose_pair(r + 1)
-                if r > 0:
-                    quantise_step(r - 1)
+                    pieces = transpose_pair(r + 1, False)
+                quantise_step(r + LEAD - 1)
                 if g > 0 and not second_pair:
                     quantise_hidden(g - 1)
                 coming = []
                 if r + 1 < PAIRS:
                     coming.append(quantise_tile(pieces[0]))
-                regroup(r)
+                regroup(r + LEAD)
                 if r + 1 < PAIRS:
                     coming.append(quantise_tile(pieces[1]))
                 if not second_pair:
@@ -222,15 +243,14 @@ def tile_invblock_pa_kernel(tc, u_old, v_old, W1, b1, out):
                 ready = coming
                 if second_pair:
                     regroup_hidden(g, act)
-                if r % PANELS == PANELS - 1:
-                    for later in range(g + CHUNKS_AHEAD - 1, min(g + CHUNKS_AHEAD + 1, CHUNKS)):
-                        load_chunk(later)
+                for later in {0: (3, 4), PANELS: (5, 6, 7)}.get(r, ()):
+                    load_chunk(later)
             quantise_step(EARLY_STEPS - 1)
             quantise_hidden(CHUNKS - 1)
-            v_sb = keep.tile([P, B_TILES, HD], BF16)
-            nc.sync.dma_start(out=v_sb[:], in_=v_old.rearrange("(t p) h -> p t h", p=P))
 
         results = ctx.enter_context(tc.tile_pool(name="results", bufs=B_TILES * PANELS))
+        v_sb = results.tile([P, B_TILES, HD], BF16, bufs=1)
+        nc.sync.dma_start(out=v_sb[:], in_=v_old.rearrange("(t p) h -> p t h", p=P))
         psum_acc = ctx.enter_context(tc.psum_pool(name="psum_acc", bufs=1))
         acc = [
             [psum_acc.tile([P, PANEL], F32, name="acc%d%d" % (t, n)) for n in range(PANELS)]
@@ -246,6 +266,8 @@ def tile_invblock_pa_kernel(tc, u_old, v_old, W1, b1, out):
                 )
                 nc.sync.dma_start(out=out[t * P : (t + 1) * P, h_cols], in_=res[:])
 
+        steps_of = [[k for k in range(STEPS) if step_place(k)[1] == n] for n in range(PANELS)]
+
         def second_matmul(k):
             g, n = step_place(k)
             codes, scales = operand_of[k]
@@ -256,20 +278,21 @@ def tile_invblock_pa_kernel(tc, u_old, v_old, W1, b1, out):
                     lhsT_scale=v_scales[:, g, t * P : (t + 1) * P],
                     rhs=codes.bitcast(FP8X4),
                     rhs_scale=scales,
-                    start=(g == 0),
-                    stop=(g == CHUNKS - 1),
+                    start=(k == steps_of[n][0]),
+                    stop=(k == steps_of[n][-1]),
                 )
 
         regroup(EARLY_STEPS)
-        for k in range(EARLY_STEPS, STEPS):
-            g, n = step_place(k)
-            if g == 1:
-                for early in range(n, EARLY_STEPS, PANELS):
-                    second_matmul(early)
-            if k + 1 < STEPS:
-                regroup(k + 1)
-            quantise_step(k)
-            second_matmul(k)
-            if g == 1 and n > 0:
-                finish(n - 1)
+        for n in range(PANELS):
+            late = [k for k in steps_of[n] if k >= EARLY_STEPS]
+            for k in steps_of[n]:
+                if k < EARLY_STEPS:
+                    second_matmul(k)
+            for place, k in enumerate(late):
+                if k + 1 < STEPS:
+                    regroup(k + 1)
+                quantise_step(k)
+                second_matmul(k)
+                if n > 0 and place == 2:
+                    finish(n - 1)
         finish(PANELS - 1)

@@ -139,22 +139,21 @@ def tile_invblock_pa_kernel(tc, u_old, v_old, W1, b1, out):
             def empty_bank(copy, bank, dest):
                 copy(out=dest, in_=bank[:].rearrange("q c u r -> q c r u"))
 
-            def transpose_pair(r, by_half):
-                pieces, views = [], []
+            def pair_pieces():
+                pieces = []
                 for i in range(2):
                     grouped = stage1.tile([P, PACK * PANEL], BF16, align_bytes=64)
-                    views.append(grouped[:].bitcast(F32).rearrange("q (c r u) -> q c r u", c=H_PASSES, u=2))
                     pieces.append(grouped)
-                order = [(i, half) for i in range(2) for half in range(2)]
-                if by_half:
-                    order = [(i, half) for half in range(2) for i in range(2)]
+                return pieces
+
+            def transpose_pair(r, pieces, parts):
                 banks = []
-                for i, half in order:
+                for i, half in parts:
                     g, j = divmod(2 * r + i, PACK)
                     banks.append(transpose_half(lambda n: panel_of_chunk(g, n)[:, j, :], half))
-                for (i, half), bank in zip(order, banks):
-                    empty_bank(nc.scalar.copy, bank, views[i][:, 2 * half : 2 * half + 2, :, :])
-                return pieces
+                for (i, half), bank in zip(parts, banks):
+                    view = pieces[i][:].bitcast(F32).rearrange("q (c r u) -> q c r u", c=H_PASSES, u=2)
+                    empty_bank(nc.scalar.copy, bank, view[:, 2 * half : 2 * half + 2, :, :])
 
             def quantise_tile(grouped):
                 w_codes = stage1.tile([P, H_PASSES * P], U32, align_bytes=64)
@@ -197,10 +196,12 @@ def tile_invblock_pa_kernel(tc, u_old, v_old, W1, b1, out):
                 )
 
             regroup(0)
-            pieces = transpose_pair(0, True)
             regroup(1)
+            pieces = pair_pieces()
+            transpose_pair(0, pieces, [(0, 0), (1, 0)])
             quantise_step(0)
             regroup(2)
+            transpose_pair(0, pieces, [(0, 1), (1, 1)])
             quantise_step(1)
             ready = [quantise_tile(pieces[0]), quantise_tile(pieces[1])]
 
@@ -226,14 +227,19 @@ def tile_invblock_pa_kernel(tc, u_old, v_old, W1, b1, out):
             for r in range(PAIRS):
                 g, second_pair = divmod(r, 2)
                 if r + 1 < PAIRS:
-                    pieces = transpose_pair(r + 1, False)
+                    pieces = pair_pieces()
+                    transpose_pair(r + 1, pieces, [(0, 0), (0, 1), (1, 0), (1, 1)])
                 quantise_step(r + LEAD - 1)
                 if g > 0 and not second_pair:
-                    quantise_hidden(g - 1)
+                    regroup_hidden(g - 1, act)
                 coming = []
                 if r + 1 < PAIRS:
                     coming.append(quantise_tile(pieces[0]))
                 regroup(r + LEAD)
+                if r == PAIRS - 1:
+                    regroup(EARLY_STEPS)
+                if g > 0 and not second_pair:
+                    quantise_hidden(g - 1)
                 if r + 1 < PAIRS:
                     coming.append(quantise_tile(pieces[1]))
                 if not second_pair:
@@ -241,11 +247,11 @@ def tile_invblock_pa_kernel(tc, u_old, v_old, W1, b1, out):
                 hidden_tile(2 * r, ready[0], act)
                 hidden_tile(2 * r + 1, ready[1], act)
                 ready = coming
-                if second_pair:
-                    regroup_hidden(g, act)
                 for later in {0: (3, 4), PANELS: (5, 6, 7)}.get(r, ()):
                     load_chunk(later)
             quantise_step(EARLY_STEPS - 1)
+            regroup_hidden(CHUNKS - 1, act)
+            regroup(EARLY_STEPS + 1)
             quantise_hidden(CHUNKS - 1)
 
         results = ctx.enter_context(tc.tile_pool(name="results", bufs=B_TILES * PANELS))
@@ -282,17 +288,16 @@ def tile_invblock_pa_kernel(tc, u_old, v_old, W1, b1, out):
                     stop=(k == steps_of[n][-1]),
                 )
 
-        regroup(EARLY_STEPS)
         for n in range(PANELS):
             late = [k for k in steps_of[n] if k >= EARLY_STEPS]
             for k in steps_of[n]:
                 if k < EARLY_STEPS:
                     second_matmul(k)
             for place, k in enumerate(late):
-                if k + 1 < STEPS:
-                    regroup(k + 1)
+                if k + 2 < STEPS:
+                    regroup(k + 2)
                 quantise_step(k)
                 second_matmul(k)
-                if n > 0 and place == 2:
+                if n > 0 and place == len(late) - 1:
                     finish(n - 1)
         finish(PANELS - 1)

@@ -31,7 +31,7 @@ PASSING = (0, 1, 3, 5)
 STAYING = (2, 4, 6, 7)
 LEAD = 3
 EARLY_STEPS = PAIRS + LEAD
-VECTOR_COLS_PHASE1 = 416
+VECTOR_COLS_PHASE1 = 400
 VECTOR_COLS_FIRST = 320
 VECTOR_COLS_PHASE2 = 192
 
@@ -91,7 +91,6 @@ def tile_invblock_pa_kernel(tc, u_old, v_old, W1, b1, out):
         u_scales = keep.tile([P, H_PASSES * B], U8, align_bytes=64)
         v_codes = keep.tile([P, CHUNKS, B], U32, align_bytes=64)
         v_scales = keep.tile([P, CHUNKS, B], U8, align_bytes=64)
-        bias = keep.tile([P, F_TILES], F32)
         early_codes = keep.tile([P, EARLY_STEPS, PANEL], U32, align_bytes=64)
         early_scales = keep.tile([P, EARLY_STEPS, PANEL], U8, align_bytes=64)
 
@@ -176,7 +175,7 @@ def tile_invblock_pa_kernel(tc, u_old, v_old, W1, b1, out):
                         start=(c == 0),
                         stop=(c == H_PASSES - 1),
                     )
-                nc.scalar.activation(out=act[:, i % PACK, :], in_=hid[:], func=TANH, bias=bias[:, i : i + 1], scale=1.0)
+                nc.scalar.activation(out=act[:, i % PACK, :], in_=hid[:], func=TANH, bias=bias_bf[:, i // PACK, i % PACK : i % PACK + 1], scale=1.0)
 
             v_grouped_of = {}
 
@@ -217,7 +216,6 @@ def tile_invblock_pa_kernel(tc, u_old, v_old, W1, b1, out):
                 for half, copy in enumerate((nc.scalar.copy, nc.vector.tensor_copy)):
                     view = u_pieces[half][:].bitcast(F32).rearrange("q (c t r u) -> q c t r u", c=2, t=B_TILES, u=2)
                     empty_bank(copy, u_banks[2 * t + half], view[:, :, t, :, :])
-            nc.vector.tensor_copy(out=bias[:], in_=bias_bf[:].rearrange("p g j -> p (g j)"))
             for half in range(2):
                 cols = slice(half * PANEL, (half + 1) * PANEL)
                 nc.vector.quantize_mx(

@@ -31,7 +31,8 @@ PASSING = (0, 1, 3, 5)
 STAYING = (2, 4, 6, 7)
 LEAD = 3
 EARLY_STEPS = PAIRS + LEAD
-VECTOR_COLS_PHASE1 = 400
+VECTOR_COLS_PHASE1 = 416
+TENSOR_COLS = 128
 VECTOR_COLS_FIRST = 320
 VECTOR_COLS_PHASE2 = 192
 
@@ -56,6 +57,8 @@ def tile_invblock_pa_kernel(tc, u_old, v_old, W1, b1, out):
 
         ident = keep.tile([P, P], F32)
         make_identity(nc, ident[:])
+        ident_bf = keep.tile([P, P], BF16)
+        make_identity(nc, ident_bf[:])
         bias_bf = keep.tile([P, CHUNKS, PACK], BF16)
         nc.scalar.dma_start(out=bias_bf[:], in_=b1.rearrange("(g p j) -> p g j", p=P, j=PACK))
         warm = keep.tile([P, 1], F32)
@@ -97,10 +100,31 @@ def tile_invblock_pa_kernel(tc, u_old, v_old, W1, b1, out):
         grouped_of = {}
         operand_of = {}
 
+        def regroup_early(k, psum_g):
+            g, n = step_place(k)
+            rows = panel_of_chunk(g, n)
+            grouped = stage2.tile([P, PANEL, PACK], BF16, name="grouped", align_bytes=64)
+            bank = psum_g.tile([P, TENSOR_COLS, PACK], BF16)
+            split = PANEL - TENSOR_COLS
+            for j in range(0, PACK, 2):
+                nc.tensor.matmul(
+                    out=bank[:, :, j : j + 2],
+                    lhsT=ident_bf[:],
+                    rhs=rows[:, j : j + 2, split:PANEL].rearrange("p t c -> p c t"),
+                    start=True,
+                    stop=True,
+                )
+            nc.scalar.copy(out=grouped[:, split:PANEL, :], in_=bank[:])
+            nc.vector.tensor_copy(
+                out=grouped[:, 0:split, :].rearrange("p (c i) t -> p c t i", i=4),
+                in_=rows[:, :, 0:split].rearrange("p t (c i) -> p c t i", i=4),
+            )
+            grouped_of[k] = grouped
+
         def regroup(k):
             g, n = step_place(k)
             rows = panel_of_chunk(g, n)
-            grouped = stage2.tile([P, PANEL, PACK], BF16, align_bytes=64)
+            grouped = stage2.tile([P, PANEL, PACK], BF16, name="grouped", align_bytes=64)
             split = VECTOR_COLS_FIRST if k == 0 else VECTOR_COLS_PHASE1 if k < EARLY_STEPS else VECTOR_COLS_PHASE2
             for copy, cols in ((nc.vector.tensor_copy, slice(0, split)), (nc.scalar.copy, slice(split, PANEL))):
                 copy(
@@ -124,7 +148,8 @@ def tile_invblock_pa_kernel(tc, u_old, v_old, W1, b1, out):
         with ExitStack() as phase1:
             stage1 = phase1.enter_context(tc.tile_pool(name="stage1", bufs=4))
             hidden_sb = phase1.enter_context(tc.tile_pool(name="hidden_sb", bufs=2))
-            psum_t = phase1.enter_context(tc.psum_pool(name="psum_t", bufs=6))
+            psum_t = phase1.enter_context(tc.psum_pool(name="psum_t", bufs=5))
+            psum_g = phase1.enter_context(tc.psum_pool(name="psum_g", bufs=1))
             psum_h = phase1.enter_context(tc.psum_pool(name="psum_h", bufs=2))
 
             def transpose_half(rows_of, half):
@@ -233,7 +258,7 @@ def tile_invblock_pa_kernel(tc, u_old, v_old, W1, b1, out):
                 coming = []
                 if r + 1 < PAIRS:
                     coming.append(quantise_tile(pieces[0]))
-                regroup(r + LEAD)
+                regroup_early(r + LEAD, psum_g)
                 if r == PAIRS - 1:
                     regroup(EARLY_STEPS)
                 if g > 0 and not second_pair:
@@ -252,7 +277,7 @@ def tile_invblock_pa_kernel(tc, u_old, v_old, W1, b1, out):
             regroup(EARLY_STEPS + 1)
             quantise_hidden(CHUNKS - 1)
 
-        results = ctx.enter_context(tc.tile_pool(name="results", bufs=B_TILES * PANELS))
+        results = ctx.enter_context(tc.tile_pool(name="results", bufs=B_TILES * PANELS + 1))
         v_sb = results.tile([P, B_TILES, HD], BF16, bufs=1)
         nc.sync.dma_start(out=v_sb[:], in_=v_old.rearrange("(t p) h -> p t h", p=P))
         psum_acc = ctx.enter_context(tc.psum_pool(name="psum_acc", bufs=1))
@@ -261,14 +286,18 @@ def tile_invblock_pa_kernel(tc, u_old, v_old, W1, b1, out):
             for t in range(B_TILES)
         ]
 
-        def finish(n):
-            h_cols = slice(n * PANEL, (n + 1) * PANEL)
-            for t in range(B_TILES):
-                res = results.tile([P, PANEL], F32)
-                nc.vector.scalar_tensor_tensor(
-                    out=res[:], in0=acc[t][n][:], scalar=STEP, in1=v_sb[:, t, h_cols], op0=MULT, op1=ADD
-                )
-                nc.sync.dma_start(out=out[t * P : (t + 1) * P, h_cols], in_=res[:])
+        def finish(t, n, first, width):
+            h_cols = slice(n * PANEL + first, n * PANEL + first + width)
+            res = results.tile([P, PANEL], F32)
+            nc.vector.scalar_tensor_tensor(
+                out=res[:, 0:width],
+                in0=acc[t][n][:, first : first + width],
+                scalar=STEP,
+                in1=v_sb[:, t, h_cols],
+                op0=MULT,
+                op1=ADD,
+            )
+            nc.sync.dma_start(out=out[t * P : (t + 1) * P, h_cols], in_=res[:, 0:width])
 
         steps_of = [[k for k in range(STEPS) if step_place(k)[1] == n] for n in range(PANELS)]
 
@@ -296,6 +325,7 @@ def tile_invblock_pa_kernel(tc, u_old, v_old, W1, b1, out):
                     regroup(k + 2)
                 quantise_step(k)
                 second_matmul(k)
-                if n > 0 and place == len(late) - 1:
-                    finish(n - 1)
-        finish(PANELS - 1)
+                if n > 0 and place >= len(late) - B_TILES:
+                    finish(place - (len(late) - B_TILES), n - 1, 0, PANEL)
+        finish(0, PANELS - 1, 0, PANEL)
+        finish(1, PANELS - 1, 0, PANEL)

from contextlib import ExitStack

import concourse.mybir as mybir
from concourse.masks import make_identity

F32 = mybir.dt.float32
BF16 = mybir.dt.bfloat16
U32 = mybir.dt.uint32
U8 = mybir.dt.uint8
FP8X4 = mybir.dt.float8_e4m3fn_x4
TANH = mybir.ActivationFunctionType.Tanh
MULT = mybir.AluOpType.mult
ADD = mybir.AluOpType.add

B, HD, F = 256, 2048, 4096
STEP = 0.1
FLOPS = 2 * 2 * B * HD * F

P = 128
PACK = 4
K_PASS = P * PACK
B_TILES = B // P
H_PASSES = HD // K_PASS
CHUNKS = F // K_PASS
F_TILES = CHUNKS * PACK
PAIRS = F_TILES // 2
PANEL = 512
PANELS = HD // PANEL
STEPS = CHUNKS * PANELS
PASSING = (0, 1, 3, 5)
STAYING = (2, 4, 6, 7)
LEAD = 3
EARLY_STEPS = PAIRS + LEAD
VECTOR_COLS_PHASE1 = 416
TENSOR_COLS = 128
VECTOR_COLS_FIRST = 320
VECTOR_COLS_PHASE2 = 192


def step_place(k):
    passing_steps = len(PASSING) * PANELS
    if k < passing_steps:
        place, n = divmod(k, PANELS)
        return PASSING[place], n
    n, place = divmod(k - passing_steps, len(STAYING))
    return STAYING[place], n


def tile_invblock_pa_kernel(tc, u_old, v_old, W1, b1, out):
    nc = tc.nc
    with ExitStack() as ctx:
        ctx.enter_context(tc.manual_schedule())
        passing = ctx.enter_context(tc.tile_pool(name="passing", bufs=2))
        staying = ctx.enter_context(tc.tile_pool(name="staying", bufs=len(STAYING)))
        keep = ctx.enter_context(tc.tile_pool(name="keep", bufs=1))
        stage2 = ctx.enter_context(tc.tile_pool(name="stage2", bufs=4))

        ident = keep.tile([P, P], F32)
        make_identity(nc, ident[:])
        ident_bf = keep.tile([P, P], BF16)
        make_identity(nc, ident_bf[:])
        bias_bf = keep.tile([P, CHUNKS, PACK], BF16)
        nc.scalar.dma_start(out=bias_bf[:], in_=b1.rearrange("(g p j) -> p g j", p=P, j=PACK))
        warm = keep.tile([P, 1], F32)
        nc.scalar.activation(out=warm[:], in_=ident[:, 0:1], func=TANH)
        w_sb = {}

        def load_chunk(g):
            pool = passing if g in PASSING else staying
            rows = W1[g * K_PASS : (g + 1) * K_PASS, :].rearrange("(p j) h -> p j h", j=PACK)
            if g == 0:
                w = pool.tile([P, PANELS, PACK, PANEL], BF16)
                for n in range(PANELS):
                    nc.sync.dma_start(out=w[:, n, :, :], in_=rows[:, :, n * PANEL : (n + 1) * PANEL])
            else:
                w = pool.tile([P, PACK, HD], BF16)
                for first in range(0, PACK, 2):
                    nc.sync.dma_start(out=w[:, first : first + 2, :], in_=rows[:, first : first + 2, :])
            w_sb[g] = w

        def panel_of_chunk(g, n):
            if g == 0:
                return w_sb[g][:, n, :, :]
            return w_sb[g][:, :, n * PANEL : (n + 1) * PANEL]

        load_chunk(0)
        u_sb = keep.tile([P, B_TILES, HD], BF16)
        for t in range(B_TILES):
            nc.sync.dma_start(out=u_sb[:, t, :], in_=u_old[t * P : (t + 1) * P, :])
        load_chunk(1)
        load_chunk(2)

        u_codes = keep.tile([P, H_PASSES * B], U32, align_bytes=64)
        u_scales = keep.tile([P, H_PASSES * B], U8, align_bytes=64)
        v_codes = keep.tile([P, CHUNKS, B], U32, align_bytes=64)
        v_scales = keep.tile([P, CHUNKS, B], U8, align_bytes=64)
        early_codes = keep.tile([P, EARLY_STEPS, PANEL], U32, align_bytes=64)
        early_scales = keep.tile([P, EARLY_STEPS, PANEL], U8, align_bytes=64)

        grouped_of = {}
        operand_of = {}

        def regroup_early(k, psum_g):
            g, n = step_place(k)
            rows = panel_of_chunk(g, n)
            grouped = stage2.tile([P, PANEL, PACK], BF16, name="grouped", align_bytes=64)
            bank = psum_g.tile([P, TENSOR_COLS, PACK], BF16)
            split = PANEL - TENSOR_COLS
            for j in range(0, PACK, 2):
                nc.tensor.matmul(
                    out=bank[:, :, j : j + 2],
                    lhsT=ident_bf[:],
                    rhs=rows[:, j : j + 2, split:PANEL].rearrange("p t c -> p c t"),
                    start=True,
                    stop=True,
                )
            nc.scalar.copy(out=grouped[:, split:PANEL, :], in_=bank[:])
            nc.vector.tensor_copy(
                out=grouped[:, 0:split, :].rearrange("p (c i) t -> p c t i", i=4),
                in_=rows[:, :, 0:split].rearrange("p t (c i) -> p c t i", i=4),
            )
            grouped_of[k] = grouped

        def regroup(k):
            g, n = step_place(k)
            rows = panel_of_chunk(g, n)
            grouped = stage2.tile([P, PANEL, PACK], BF16, name="grouped", align_bytes=64)
            split = VECTOR_COLS_FIRST if k == 0 else VECTOR_COLS_PHASE1 if k < EARLY_STEPS else VECTOR_COLS_PHASE2
            for copy, cols in ((nc.vector.tensor_copy, slice(0, split)), (nc.scalar.copy, slice(split, PANEL))):
                copy(
                    out=grouped[:, cols, :].rearrange("p (c i) t -> p c t i", i=4),
                    in_=rows[:, :, cols].rearrange("p t (c i) -> p c t i", i=4),
                )
            grouped_of[k] = grouped

        def quantise_step(k):
            if k < EARLY_STEPS:
                codes, scales = early_codes[:, k, :], early_scales[:, k, :]
            else:
                late_codes = stage2.tile([P, PANEL], U32, align_bytes=64)
                late_scales = stage2.tile([P, PANEL], U8, align_bytes=64)
                codes, scales = late_codes[:], late_scales[:]
            nc.vector.quantize_mx(
                out=codes.bitcast(FP8X4), scales=scales, in_=grouped_of[k][:].rearrange("p h t -> p (h t)")
            )
            operand_of[k] = (codes, scales)

        with ExitStack() as phase1:
            stage1 = phase1.enter_context(tc.tile_pool(name="stage1", bufs=4))
            hidden_sb = phase1.enter_context(tc.tile_pool(name="hidden_sb", bufs=2))
            psum_t = phase1.enter_context(tc.psum_pool(name="psum_t", bufs=5))
            psum_g = phase1.enter_context(tc.psum_pool(name="psum_g", bufs=1))
            psum_h = phase1.enter_context(tc.psum_pool(name="psum_h", bufs=2))

            def transpose_half(rows_of, half):
                bank = psum_t.tile([P, 2, 2, P], F32)
                for c2 in range(2):
                    words = rows_of(2 * half + c2).bitcast(F32)
                    for u in range(2):
                        nc.tensor.transpose(bank[:, c2, u, :], words[:, u * P : (u + 1) * P], ident[:])
                return bank

            def empty_bank(copy, bank, dest):
                copy(out=dest, in_=bank[:].rearrange("q c u r -> q c r u"))

            def pair_pieces():
                pieces = []
                for i in range(2):
                    grouped = stage1.tile([P, PACK * PANEL], BF16, align_bytes=64)
                    pieces.append(grouped)
                return pieces

            def transpose_pair(r, pieces, parts):
                banks = []
                for i, half in parts:
                    g, j = divmod(2 * r + i, PACK)
                    banks.append(transpose_half(lambda n: panel_of_chunk(g, n)[:, j, :], half))
                for (i, half), bank in zip(parts, banks):
                    view = pieces[i][:].bitcast(F32).rearrange("q (c r u) -> q c r u", c=H_PASSES, u=2)
                    empty_bank(nc.scalar.copy, bank, view[:, 2 * half : 2 * half + 2, :, :])

            def quantise_tile(grouped):
                w_codes = stage1.tile([P, H_PASSES * P], U32, align_bytes=64)
                w_scales = stage1.tile([P, H_PASSES * P], U8, align_bytes=64)
                nc.vector.quantize_mx(out=w_codes[:].bitcast(FP8X4), scales=w_scales[:], in_=grouped[:])
                return w_codes, w_scales

            def hidden_tile(i, operand, act):
                w_codes, w_scales = operand
                hid = psum_h.tile([P, B], F32)
                for c in range(H_PASSES):
                    f_cols = slice(c * P, (c + 1) * P)
                    b_cols = slice(c * B, (c + 1) * B)
                    nc.tensor.matmul_mx(
                        out=hid[:],
                        lhsT=w_codes[:, f_cols].bitcast(FP8X4),
                        lhsT_scale=w_scales[:, f_cols],
                        rhs=u_codes[:, b_cols].bitcast(FP8X4),
                        rhs_scale=u_scales[:, b_cols],
                        start=(c == 0),
                        stop=(c == H_PASSES - 1),
                    )
                nc.scalar.activation(out=act[:, i % PACK, :], in_=hid[:], func=TANH, bias=bias_bf[:, i // PACK, i % PACK : i % PACK + 1], scale=1.0)

            v_grouped_of = {}

            def regroup_hidden(g, act):
                v_grouped = hidden_sb.tile([P, B, PACK], BF16, align_bytes=64)
                nc.vector.tensor_copy(
                    out=v_grouped[:].rearrange("p (c i) t -> p c t i", i=4),
                    in_=act[:].rearrange("p t (c i) -> p c t i", i=4),
                )
                v_grouped_of[g] = v_grouped

            def quantise_hidden(g):
                nc.vector.quantize_mx(
                    out=v_codes[:, g, :].bitcast(FP8X4),
                    scales=v_scales[:, g, :],
                    in_=v_grouped_of[g][:].rearrange("p b t -> p (b t)"),
                )

            regroup(0)
            regroup(1)
            pieces = pair_pieces()
            transpose_pair(0, pieces, [(0, 0), (1, 0)])
            quantise_step(0)
            regroup(2)
            transpose_pair(0, pieces, [(0, 1), (1, 1)])
            quantise_step(1)
            ready = [quantise_tile(pieces[0]), quantise_tile(pieces[1])]

            u_banks = []
            for t in range(B_TILES):
                for half in range(2):
                    u_banks.append(transpose_half(lambda n: u_sb[:, t, n * PANEL : (n + 1) * PANEL], half))
            u_pieces = []
            for half in range(2):
                grouped = stage1.tile([P, PACK * PANEL], BF16, align_bytes=64)
                u_pieces.append(grouped)
            for t in range(B_TILES):
                for half, copy in enumerate((nc.scalar.copy, nc.vector.tensor_copy)):
                    view = u_pieces[half][:].bitcast(F32).rearrange("q (c t r u) -> q c t r u", c=2, t=B_TILES, u=2)
                    empty_bank(copy, u_banks[2 * t + half], view[:, :, t, :, :])
            for half in range(2):
                cols = slice(half * PANEL, (half + 1) * PANEL)
                nc.vector.quantize_mx(
                    out=u_codes[:, cols].bitcast(FP8X4), scales=u_scales[:, cols], in_=u_pieces[half][:]
                )

            for r in range(PAIRS):
                g, second_pair = divmod(r, 2)
                if r + 1 < PAIRS:
                    pieces = pair_pieces()
                    transpose_pair(r + 1, pieces, [(0, 0), (0, 1), (1, 0), (1, 1)])
                quantise_step(r + LEAD - 1)
                if g > 0 and not second_pair:
                    regroup_hidden(g - 1, act)
                coming = []
                if r + 1 < PAIRS:
                    coming.append(quantise_tile(pieces[0]))
                regroup_early(r + LEAD, psum_g)
                if r == PAIRS - 1:
                    regroup(EARLY_STEPS)
                if g > 0 and not second_pair:
                    quantise_hidden(g - 1)
                if r + 1 < PAIRS:
                    coming.append(quantise_tile(pieces[1]))
                if not second_pair:
                    act = hidden_sb.tile([P, PACK, B], BF16)
                hidden_tile(2 * r, ready[0], act)
                hidden_tile(2 * r + 1, ready[1], act)
                ready = coming
                for later in {0: (3, 4), PANELS: (5, 6, 7)}.get(r, ()):
                    load_chunk(later)
            quantise_step(EARLY_STEPS - 1)
            regroup_hidden(CHUNKS - 1, act)
            regroup(EARLY_STEPS + 1)
            quantise_hidden(CHUNKS - 1)

        results = ctx.enter_context(tc.tile_pool(name="results", bufs=B_TILES * PANELS + 1))
        v_sb = results.tile([P, B_TILES, HD], BF16, bufs=1)
        nc.sync.dma_start(out=v_sb[:], in_=v_old.rearrange("(t p) h -> p t h", p=P))
        psum_acc = ctx.enter_context(tc.psum_pool(name="psum_acc", bufs=1))
        acc = [
            [psum_acc.tile([P, PANEL], F32, name="acc%d%d" % (t, n)) for n in range(PANELS)]
            for t in range(B_TILES)
        ]

        def finish(t, n, first, width):
            h_cols = slice(n * PANEL + first, n * PANEL + first + width)
            res = results.tile([P, PANEL], F32)
            nc.vector.scalar_tensor_tensor(
                out=res[:, 0:width],
                in0=acc[t][n][:, first : first + width],
                scalar=STEP,
                in1=v_sb[:, t, h_cols],
                op0=MULT,
                op1=ADD,
            )
            nc.sync.dma_start(out=out[t * P : (t + 1) * P, h_cols], in_=res[:, 0:width])

        steps_of = [[k for k in range(STEPS) if step_place(k)[1] == n] for n in range(PANELS)]

        def second_matmul(k):
            g, n = step_place(k)
            codes, scales = operand_of[k]
            for t in range(B_TILES):
                nc.tensor.matmul_mx(
                    out=acc[t][n][:],
                    lhsT=v_codes[:, g, t * P : (t + 1) * P].bitcast(FP8X4),
                    lhsT_scale=v_scales[:, g, t * P : (t + 1) * P],
                    rhs=codes.bitcast(FP8X4),
                    rhs_scale=scales,
                    start=(k == steps_of[n][0]),
                    stop=(k == steps_of[n][-1]),
                )

        for n in range(PANELS):
            late = [k for k in steps_of[n] if k >= EARLY_STEPS]
            for k in steps_of[n]:
                if k < EARLY_STEPS:
                    second_matmul(k)
            for place, k in enumerate(late):
                if k + 2 < STEPS:
                    regroup(k + 2)
                quantise_step(k)
                second_matmul(k)
                if n > 0 and place >= len(late) - B_TILES:
                    finish(place - (len(late) - B_TILES), n - 1, 0, PANEL)
        finish(0, PANELS - 1, 0, PANEL)
        finish(1, PANELS - 1, 0, PANEL)
